import numpy as np
import ml_dtypes

BF16 = ml_dtypes.bfloat16


def bf(x):
    return np.asarray(x, np.float32).astype(BF16)


def f32(x):
    return np.asarray(x, np.float32)


def f64(x):
    return np.asarray(x).astype(np.float64)


def striped(idx):
    return np.tile(idx.reshape(-1, 16).T, (8, 1))


B, NETS, D, O, K, S, N, ITERS = 512, 8, 128, 8, 32, 2048, 256, 3


def squash_scale(sq):
    return np.sqrt(sq) / (1.0 + sq)


def setup_inputs():
    amp = np.random.uniform(0.5, 1.5, (B, NETS, 1))
    h = 0.2 * amp * np.abs(np.random.standard_normal((B, NETS, D)))
    return {"base": f32(0.2 * np.random.standard_normal((B, S))), "h": bf(h.reshape(B, NETS * D)), "rw": bf(np.random.standard_normal((NETS, D, N))), "offs": striped(np.random.permutation(S)[:N])}


def reference(base, h, rw, offs):
    idx = offs[:16].T.reshape(-1)
    hh = f64(h).reshape(B, NETS, D)
    q = (hh * hh).sum(axis=2)
    p = np.einsum("bnd,ndm->bnm", hh, f64(rw)) * squash_scale(q)[:, :, None]
    p = p.reshape(B, NETS, O, K)
    logit = np.zeros((B, NETS, O))
    v = None
    for it in range(ITERS):
        e = np.exp(logit)
        prob = e / e.sum(axis=2, keepdims=True)
        t = (prob[:, :, :, None] * p).sum(axis=1)
        r = (t * t).sum(axis=2, keepdims=True)
        v = t * squash_scale(r)
        if it + 1 < ITERS:
            logit = logit + (p * v[:, None, :, :]).sum(axis=3)
    out = f64(base).copy()
    out[:, idx] = v.reshape(B, N)
    return out

@@ -1,0 +1,131 @@
+import concourse.mybir as mybir
+from concourse.masks import make_identity
+
+F32 = mybir.dt.float32
+BF16 = mybir.dt.bfloat16
+U16 = mybir.dt.uint16
+ACT = mybir.ActivationFunctionType
+ALU = mybir.AluOpType
+AX = mybir.AxisListType
+
+P = 128
+B, NETS, D, O, K, S, N, PASSES = 512, 8, 128, 8, 32, 2048, 256, 3
+BLOCKS = B // P
+FLOPS = 2 * B * NETS * D * N
+
+
+def squash_scale(nc, pool, sq_norm):
+    root = pool.tile([P, 8], F32, name="root")
+    nc.scalar.activation(root[:], sq_norm[:], ACT.Sqrt)
+    denom = pool.tile([P, 8], F32, name="denom")
+    nc.vector.tensor_scalar_add(denom[:], sq_norm[:], 1.0)
+    nc.vector.reciprocal(denom[:], denom[:])
+    scale = pool.tile([P, 8], F32, name="scale")
+    nc.vector.tensor_mul(scale[:], root[:], denom[:])
+    return scale
+
+
+def tile_netgram_kernel(tc, base, h, rw, offs, out):
+    nc = tc.nc
+    with (
+        tc.tile_pool(name="held", bufs=1) as held,
+        tc.tile_pool(name="windows", bufs=BLOCKS) as windows,
+        tc.tile_pool(name="big", bufs=2) as big,
+        tc.tile_pool(name="small", bufs=2) as small,
+        tc.psum_pool(name="flip", bufs=2) as flip,
+        tc.psum_pool(name="votes", bufs=4) as votes,
+    ):
+        offsets = held.tile([P, N // 16], U16, name="offsets")
+        nc.sync.dma_start(offsets[:], offs)
+        rw_sb = held.tile([P, NETS, N], BF16, name="rw_sb")
+        nc.sync.dma_start(rw_sb[:], rw.rearrange("n d m -> d n m"))
+        identity = held.tile([P, P], BF16, name="identity")
+        make_identity(nc, identity[:])
+
+        for blk in range(BLOCKS):
+            rows = slice(blk * P, (blk + 1) * P)
+            h_sb = big.tile([P, NETS * D], BF16, name="h_sb")
+            nc.sync.dma_start(h_sb[:], h[rows, :])
+            window = windows.tile([P, S], F32, name="window")
+            nc.sync.dma_start(window[:], base[rows, :])
+
+            q = small.tile([P, NETS], F32, name="q")
+            squares = small.tile([P, D], F32, name="squares")
+            for n in range(NETS):
+                nc.scalar.activation(
+                    squares[:], h_sb[:, n * D : (n + 1) * D], ACT.Square, accum_out=q[:, n : n + 1]
+                )
+            s = squash_scale(nc, small, q)
+
+            hT_ps = flip.tile([P, NETS * P], BF16, name="hT_ps")
+            for n in range(NETS):
+                nc.tensor.transpose(hT_ps[:, n * P : (n + 1) * P], h_sb[:, n * D : (n + 1) * D], identity[:])
+            hT = big.tile([P, NETS * P], BF16, name="hT")
+            nc.scalar.copy(hT[:], hT_ps[:])
+
+            p = big.tile([P, NETS, N], F32, name="p")
+            for pair in range(NETS // 2):
+                votes_ps = votes.tile([P, 2 * N], F32, name="votes_ps")
+                for half in range(2):
+                    n = 2 * pair + half
+                    nc.tensor.matmul(
+                        votes_ps[:, half * N : (half + 1) * N],
+                        lhsT=hT[:, n * P : (n + 1) * P],
+                        rhs=rw_sb[:, n, :],
+                        start=True,
+                        stop=True,
+                    )
+                    nc.scalar.activation(
+                        p[:, n, :], votes_ps[:, half * N : (half + 1) * N], ACT.Copy, scale=s[:, n : n + 1]
+                    )
+
+            logit = small.tile([P, NETS, O], F32, name="logit")
+            for turn in range(PASSES):
+                t = small.tile([P, O, K], F32, name="t")
+                t_flat = t[:].rearrange("p o k -> p (o k)")
+                if turn == 0:
+                    nc.vector.tensor_reduce(t_flat, p[:].rearrange("p n m -> p m n"), axis=AX.X, op=ALU.add)
+                    nc.vector.tensor_scalar_mul(t_flat, t_flat, 1.0 / O)
+                else:
+                    top = small.tile([P, NETS], F32, name="top")
+                    nc.vector.tensor_reduce(top[:], logit[:], axis=AX.X, op=ALU.max)
+                    prob = small.tile([P, NETS, O], F32, name="prob")
+                    nc.vector.tensor_sub(prob[:], logit[:], top[:].unsqueeze(2).to_broadcast([P, NETS, O]))
+                    nc.scalar.activation(prob[:], prob[:], ACT.Exp)
+                    total = small.tile([P, NETS], F32, name="total")
+                    nc.vector.tensor_reduce(total[:], prob[:], axis=AX.X, op=ALU.add)
+                    nc.vector.reciprocal(total[:], total[:])
+                    nc.vector.tensor_mul(prob[:], prob[:], total[:].unsqueeze(2).to_broadcast([P, NETS, O]))
+                    weighted = big.tile([P, NETS, N], F32, name="weighted")
+                    nc.vector.tensor_mul(
+                        weighted[:].rearrange("p n (o k) -> p (n o) k", k=K),
+                        p[:].rearrange("p n (o k) -> p (n o) k", k=K),
+                        prob[:].rearrange("p n o -> p (n o)").unsqueeze(2).to_broadcast([P, NETS * O, K]),
+                    )
+                    nc.vector.tensor_reduce(t_flat, weighted[:].rearrange("p n m -> p m n"), axis=AX.X, op=ALU.add)
+
+                t_sq = small.tile([P, O, K], F32, name="t_sq")
+                nc.vector.tensor_mul(t_sq[:], t[:], t[:])
+                r = small.tile([P, O], F32, name="r")
+                nc.vector.tensor_reduce(r[:], t_sq[:], axis=AX.X, op=ALU.add)
+                g = squash_scale(nc, small, r)
+                v = small.tile([P, O, K], F32, name="v")
+                nc.vector.tensor_mul(v[:], t[:], g[:].unsqueeze(2).to_broadcast([P, O, K]))
+
+                if turn + 1 < PASSES:
+                    agree = big.tile([P, NETS, N], F32, name="agree")
+                    nc.vector.tensor_mul(
+                        agree[:],
+                        p[:],
+                        v[:].rearrange("p o k -> p (o k)").unsqueeze(1).to_broadcast([P, NETS, N]),
+                    )
+                    agree_by_k = agree[:].rearrange("p n (o k) -> p n o k", k=K)
+                    if turn == 0:
+                        nc.vector.tensor_reduce(logit[:], agree_by_k, axis=AX.X, op=ALU.add)
+                    else:
+                        step = small.tile([P, NETS, O], F32, name="step")
+                        nc.vector.tensor_reduce(step[:], agree_by_k, axis=AX.X, op=ALU.add)
+                        nc.vector.tensor_add(logit[:], logit[:], step[:])
+
+            nc.scalar.activation(window[:].indirect(offsets[:]), v[:].rearrange("p o k -> p (o k)"), ACT.Copy)
+            nc.sync.dma_start(out[rows, :], window[:])

@@ -14,13 +14,13 @@ BLOCKS = B // P
 FLOPS = 2 * B * NETS * D * N
 
 
-def squash_scale(nc, pool, sq_norm):
-    root = pool.tile([P, 8], F32, name="root")
-    nc.scalar.activation(root[:], sq_norm[:], ACT.Sqrt)
-    denom = pool.tile([P, 8], F32, name="denom")
-    nc.vector.tensor_scalar_add(denom[:], sq_norm[:], 1.0)
+def squash_scale(nc, pool, sq_norm, width):
+    root = pool.tile([P, width], F32, name="root")
+    nc.scalar.activation(root[:], sq_norm, ACT.Sqrt)
+    denom = pool.tile([P, width], F32, name="denom")
+    nc.vector.tensor_scalar_add(denom[:], sq_norm, 1.0)
     nc.vector.reciprocal(denom[:], denom[:])
-    scale = pool.tile([P, 8], F32, name="scale")
+    scale = pool.tile([P, width], F32, name="scale")
     nc.vector.tensor_mul(scale[:], root[:], denom[:])
     return scale
 
@@ -29,41 +29,56 @@ def tile_netgram_kernel(tc, base, h, rw, offs, out):
     nc = tc.nc
     with (
         tc.tile_pool(name="held", bufs=1) as held,
-        tc.tile_pool(name="windows", bufs=BLOCKS) as windows,
-        tc.tile_pool(name="big", bufs=2) as big,
+        tc.tile_pool(name="per_block", bufs=BLOCKS) as per_block,
+        tc.tile_pool(name="work", bufs=2) as work,
         tc.tile_pool(name="small", bufs=2) as small,
         tc.psum_pool(name="flip", bufs=2) as flip,
-        tc.psum_pool(name="votes", bufs=4) as votes,
+        tc.psum_pool(name="votes", bufs=2) as votes,
+        tc.psum_pool(name="sums", bufs=BLOCKS) as sums,
     ):
+        h_sb = []
+        for blk in range(BLOCKS):
+            h_sb.append(per_block.tile([P, NETS * D], BF16, name="h_sb"))
+            nc.sync.dma_start(h_sb[blk][:], h[blk * P : (blk + 1) * P, :])
+        rw_sb = held.tile([P, NETS, N], BF16, name="rw_sb")
+        nc.scalar.dma_start(rw_sb[:], rw.rearrange("n d m -> d n m"))
         offsets = held.tile([P, N // 16], U16, name="offsets")
         nc.sync.dma_start(offsets[:], offs)
-        rw_sb = held.tile([P, NETS, N], BF16, name="rw_sb")
-        nc.sync.dma_start(rw_sb[:], rw.rearrange("n d m -> d n m"))
+        window = []
+        for blk in range(BLOCKS):
+            window.append(per_block.tile([P, S], F32, name="window"))
+            nc.sync.dma_start(window[blk][:], base[blk * P : (blk + 1) * P, :])
+
         identity = held.tile([P, P], BF16, name="identity")
         make_identity(nc, identity[:])
+        eye = held.tile([P, P], F32, name="eye")
+        make_identity(nc, eye[:])
+        eye_over_o = held.tile([P, P], F32, name="eye_over_o")
+        nc.gpsimd.tensor_scalar_mul(eye_over_o[:], eye[:], 1.0 / O)
 
+        def sum_over_nets(blk, terms, weights):
+            t_ps = sums.tile([P, N], F32, name="t_ps")
+            for n in range(NETS):
+                nc.tensor.matmul(t_ps[:], lhsT=weights[:], rhs=terms[:, n, :], start=(n == 0), stop=(n == NETS - 1))
+            return t_ps
+
+        p = []
         for blk in range(BLOCKS):
-            rows = slice(blk * P, (blk + 1) * P)
-            h_sb = big.tile([P, NETS * D], BF16, name="h_sb")
-            nc.sync.dma_start(h_sb[:], h[rows, :])
-            window = windows.tile([P, S], F32, name="window")
-            nc.sync.dma_start(window[:], base[rows, :])
-
             q = small.tile([P, NETS], F32, name="q")
             squares = small.tile([P, D], F32, name="squares")
             for n in range(NETS):
                 nc.scalar.activation(
-                    squares[:], h_sb[:, n * D : (n + 1) * D], ACT.Square, accum_out=q[:, n : n + 1]
+                    squares[:], h_sb[blk][:, n * D : (n + 1) * D], ACT.Square, accum_out=q[:, n : n + 1]
                 )
-            s = squash_scale(nc, small, q)
+            s = squash_scale(nc, small, q[:], NETS)
 
             hT_ps = flip.tile([P, NETS * P], BF16, name="hT_ps")
             for n in range(NETS):
-                nc.tensor.transpose(hT_ps[:, n * P : (n + 1) * P], h_sb[:, n * D : (n + 1) * D], identity[:])
-            hT = big.tile([P, NETS * P], BF16, name="hT")
-            nc.scalar.copy(hT[:], hT_ps[:])
+                nc.tensor.transpose(hT_ps[:, n * P : (n + 1) * P], h_sb[blk][:, n * D : (n + 1) * D], identity[:])
+            hT = per_block.tile([P, NETS * P], BF16, name="hT")
+            nc.vector.tensor_copy(hT[:], hT_ps[:])
 
-            p = big.tile([P, NETS, N], F32, name="p")
+            p.append(per_block.tile([P, NETS, N], F32, name="p"))
             for pair in range(NETS // 2):
                 votes_ps = votes.tile([P, 2 * N], F32, name="votes_ps")
                 for half in range(2):
@@ -76,56 +91,71 @@ def tile_netgram_kernel(tc, base, h, rw, offs, out):
                         stop=True,
                     )
                     nc.scalar.activation(
-                        p[:, n, :], votes_ps[:, half * N : (half + 1) * N], ACT.Copy, scale=s[:, n : n + 1]
+                        p[blk][:, n, :], votes_ps[:, half * N : (half + 1) * N], ACT.Copy, scale=s[:, n : n + 1]
                     )
 
-            logit = small.tile([P, NETS, O], F32, name="logit")
-            for turn in range(PASSES):
-                t = small.tile([P, O, K], F32, name="t")
-                t_flat = t[:].rearrange("p o k -> p (o k)")
-                if turn == 0:
-                    nc.vector.tensor_reduce(t_flat, p[:].rearrange("p n m -> p m n"), axis=AX.X, op=ALU.add)
-                    nc.vector.tensor_scalar_mul(t_flat, t_flat, 1.0 / O)
-                else:
-                    top = small.tile([P, NETS], F32, name="top")
-                    nc.vector.tensor_reduce(top[:], logit[:], axis=AX.X, op=ALU.max)
-                    prob = small.tile([P, NETS, O], F32, name="prob")
-                    nc.vector.tensor_sub(prob[:], logit[:], top[:].unsqueeze(2).to_broadcast([P, NETS, O]))
-                    nc.scalar.activation(prob[:], prob[:], ACT.Exp)
-                    total = small.tile([P, NETS], F32, name="total")
-                    nc.vector.tensor_reduce(total[:], prob[:], axis=AX.X, op=ALU.add)
-                    nc.vector.reciprocal(total[:], total[:])
-                    nc.vector.tensor_mul(prob[:], prob[:], total[:].unsqueeze(2).to_broadcast([P, NETS, O]))
-                    weighted = big.tile([P, NETS, N], F32, name="weighted")
+        logit = held.tile([P, BLOCKS, NETS, O], F32, name="logit")
+        for turn in range(PASSES):
+            t_ps = []
+            if turn == 0:
+                for blk in range(BLOCKS):
+                    t_ps.append(sum_over_nets(blk, p[blk], eye_over_o))
+            else:
+                rows = [P, BLOCKS * NETS, O]
+                logit_rows = logit[:].rearrange("p b n o -> p (b n) o")
+                top = small.tile([P, BLOCKS * NETS], F32, name="top")
+                nc.vector.tensor_reduce(top[:], logit_rows, axis=AX.X, op=ALU.max)
+                prob = small.tile(rows, F32, name="prob")
+                nc.vector.tensor_sub(prob[:], logit_rows, top[:].unsqueeze(2).to_broadcast(rows))
+                nc.scalar.activation(prob[:], prob[:], ACT.Exp)
+                total = small.tile([P, BLOCKS * NETS], F32, name="total")
+                nc.vector.tensor_reduce(total[:], prob[:], axis=AX.X, op=ALU.add)
+                nc.vector.reciprocal(total[:], total[:])
+                nc.vector.tensor_mul(prob[:], prob[:], total[:].unsqueeze(2).to_broadcast(rows))
+                for blk in range(BLOCKS):
+                    weighted = per_block.tile([P, NETS, N], F32, name="weighted")
                     nc.vector.tensor_mul(
                         weighted[:].rearrange("p n (o k) -> p (n o) k", k=K),
-                        p[:].rearrange("p n (o k) -> p (n o) k", k=K),
-                        prob[:].rearrange("p n o -> p (n o)").unsqueeze(2).to_broadcast([P, NETS * O, K]),
+                        p[blk][:].rearrange("p n (o k) -> p (n o) k", k=K),
+                        prob[:, blk * NETS : (blk + 1) * NETS, :]
+                        .rearrange("p n o -> p (n o)")
+                        .unsqueeze(2)
+                        .to_broadcast([P, NETS * O, K]),
                     )
-                    nc.vector.tensor_reduce(t_flat, weighted[:].rearrange("p n m -> p m n"), axis=AX.X, op=ALU.add)
+                    t_ps.append(sum_over_nets(blk, weighted, eye))
 
-                t_sq = small.tile([P, O, K], F32, name="t_sq")
-                nc.vector.tensor_mul(t_sq[:], t[:], t[:])
-                r = small.tile([P, O], F32, name="r")
+            if turn + 1 < PASSES:
+                t_sq = small.tile([P, BLOCKS * O, K], F32, name="t_sq")
+                raw = small.tile([P, BLOCKS, NETS, O], F32, name="raw")
+                for blk in range(BLOCKS):
+                    nc.scalar.activation(
+                        t_sq[:, blk * O : (blk + 1) * O, :], t_ps[blk][:].rearrange("p (o k) -> p o k", k=K), ACT.Square
+                    )
+                    agree = work.tile([P, NETS, N], F32, name="agree")
+                    nc.vector.tensor_mul(agree[:], p[blk][:], t_ps[blk][:].unsqueeze(1).to_broadcast([P, NETS, N]))
+                    nc.vector.tensor_reduce(
+                        raw[:, blk], agree[:].rearrange("p n (o k) -> p n o k", k=K), axis=AX.X, op=ALU.add
+                    )
+                r = small.tile([P, BLOCKS * O], F32, name="r")
                 nc.vector.tensor_reduce(r[:], t_sq[:], axis=AX.X, op=ALU.add)
-                g = squash_scale(nc, small, r)
-                v = small.tile([P, O, K], F32, name="v")
-                nc.vector.tensor_mul(v[:], t[:], g[:].unsqueeze(2).to_broadcast([P, O, K]))
-
-                if turn + 1 < PASSES:
-                    agree = big.tile([P, NETS, N], F32, name="agree")
-                    nc.vector.tensor_mul(
-                        agree[:],
-                        p[:],
-                        v[:].rearrange("p o k -> p (o k)").unsqueeze(1).to_broadcast([P, NETS, N]),
+                g = squash_scale(nc, small, r[:], BLOCKS * O)
+                g_for_nets = g[:].rearrange("p (b o) -> p b o", o=O).unsqueeze(2).to_broadcast([P, BLOCKS, NETS, O])
+                if turn == 0:
+                    nc.vector.tensor_mul(logit[:], raw[:], g_for_nets)
+                else:
+                    nc.vector.tensor_mul(raw[:], raw[:], g_for_nets)
+                    nc.vector.tensor_add(logit[:], logit[:], raw[:])
+            else:
+                for blk in range(BLOCKS):
+                    t_by_capsule = t_ps[blk][:].rearrange("p (o k) -> p o k", k=K)
+                    last_sq = small.tile([P, O, K], F32, name="last_sq")
+                    nc.scalar.activation(last_sq[:], t_by_capsule, ACT.Square)
+                    last_r = small.tile([P, O], F32, name="last_r")
+                    nc.vector.tensor_reduce(last_r[:], last_sq[:], axis=AX.X, op=ALU.add)
+                    last_g = squash_scale(nc, small, last_r[:], O)
+                    v = small.tile([P, O, K], F32, name="v")
+                    nc.vector.tensor_mul(v[:], t_by_capsule, last_g[:].unsqueeze(2).to_broadcast([P, O, K]))
+                    nc.scalar.activation(
+                        window[blk][:].indirect(offsets[:]), v[:].rearrange("p o k -> p (o k)"), ACT.Copy
                     )
-                    agree_by_k = agree[:].rearrange("p n (o k) -> p n o k", k=K)
-                    if turn == 0:
-                        nc.vector.tensor_reduce(logit[:], agree_by_k, axis=AX.X, op=ALU.add)
-                    else:
-                        step = small.tile([P, NETS, O], F32, name="step")
-                        nc.vector.tensor_reduce(step[:], agree_by_k, axis=AX.X, op=ALU.add)
-                        nc.vector.tensor_add(logit[:], logit[:], step[:])
-
-            nc.scalar.activation(window[:].indirect(offsets[:]), v[:].rearrange("p o k -> p (o k)"), ACT.Copy)
-            nc.sync.dma_start(out[rows, :], window[:])
+                    nc.sync.dma_start(out[blk * P : (blk + 1) * P, :], window[blk][:])

@@ -125,20 +125,30 @@ def tile_netgram_kernel(tc, base, h, rw, offs, out):
                     t_ps.append(sum_over_nets(blk, weighted, eye))
 
             if turn + 1 < PASSES:
-                t_sq = small.tile([P, BLOCKS * O, K], F32, name="t_sq")
+                r = small.tile([P, BLOCKS * O], F32, name="r")
                 raw = small.tile([P, BLOCKS, NETS, O], F32, name="raw")
+                root = small.tile([P, BLOCKS * O], F32, name="root")
+                denom = small.tile([P, BLOCKS * O], F32, name="denom")
                 for blk in range(BLOCKS):
-                    nc.scalar.activation(
-                        t_sq[:, blk * O : (blk + 1) * O, :], t_ps[blk][:].rearrange("p (o k) -> p o k", k=K), ACT.Square
-                    )
+                    for o in range(O):
+                        t_sq = small.tile([P, K], F32, name="t_sq")
+                        nc.scalar.activation(
+                            t_sq[:],
+                            t_ps[blk][:, o * K : (o + 1) * K],
+                            ACT.Square,
+                            accum_out=r[:, blk * O + o : blk * O + o + 1],
+                        )
                     agree = work.tile([P, NETS, N], F32, name="agree")
                     nc.vector.tensor_mul(agree[:], p[blk][:], t_ps[blk][:].unsqueeze(1).to_broadcast([P, NETS, N]))
+                    if blk == BLOCKS - 1:
+                        nc.scalar.activation(root[:], r[:], ACT.Sqrt)
+                        nc.scalar.activation(denom[:], r[:], ACT.Copy, bias=1.0)
+                        nc.vector.reciprocal(denom[:], denom[:])
                     nc.vector.tensor_reduce(
                         raw[:, blk], agree[:].rearrange("p n (o k) -> p n o k", k=K), axis=AX.X, op=ALU.add
                     )
-                r = small.tile([P, BLOCKS * O], F32, name="r")
-                nc.vector.tensor_reduce(r[:], t_sq[:], axis=AX.X, op=ALU.add)
-                g = squash_scale(nc, small, r[:], BLOCKS * O)
+                g = small.tile([P, BLOCKS * O], F32, name="g")
+                nc.vector.tensor_mul(g[:], root[:], denom[:])
                 g_for_nets = g[:].rearrange("p (b o) -> p b o", o=O).unsqueeze(2).to_broadcast([P, BLOCKS, NETS, O])
                 if turn == 0:
                     nc.vector.tensor_mul(logit[:], raw[:], g_for_nets)

@@ -114,14 +114,17 @@ def tile_netgram_kernel(tc, base, h, rw, offs, out):
                 nc.vector.tensor_mul(prob[:], prob[:], total[:].unsqueeze(2).to_broadcast(rows))
                 for blk in range(BLOCKS):
                     weighted = per_block.tile([P, NETS, N], F32, name="weighted")
-                    nc.vector.tensor_mul(
-                        weighted[:].rearrange("p n (o k) -> p (n o) k", k=K),
-                        p[blk][:].rearrange("p n (o k) -> p (n o) k", k=K),
-                        prob[:, blk * NETS : (blk + 1) * NETS, :]
-                        .rearrange("p n o -> p (n o)")
-                        .unsqueeze(2)
-                        .to_broadcast([P, NETS * O, K]),
-                    )
+                    nets_in_piece = 2 if blk == 0 else NETS
+                    for first in range(0, NETS, nets_in_piece):
+                        nets = slice(first, first + nets_in_piece)
+                        nc.vector.tensor_mul(
+                            weighted[:, nets, :].rearrange("p n (o k) -> p (n o) k", k=K),
+                            p[blk][:, nets, :].rearrange("p n (o k) -> p (n o) k", k=K),
+                            prob[:, blk * NETS + first : blk * NETS + first + nets_in_piece, :]
+                            .rearrange("p n o -> p (n o)")
+                            .unsqueeze(2)
+                            .to_broadcast([P, nets_in_piece * O, K]),
+                        )
                     t_ps.append(sum_over_nets(blk, weighted, eye))
 
             if turn + 1 < PASSES:
@@ -130,6 +133,8 @@ def tile_netgram_kernel(tc, base, h, rw, offs, out):
                 root = small.tile([P, BLOCKS * O], F32, name="root")
                 denom = small.tile([P, BLOCKS * O], F32, name="denom")
                 for blk in range(BLOCKS):
+                    agree = work.tile([P, NETS, N], F32, name="agree")
+                    nc.vector.tensor_mul(agree[:], p[blk][:], t_ps[blk][:].unsqueeze(1).to_broadcast([P, NETS, N]))
                     for o in range(O):
                         t_sq = small.tile([P, K], F32, name="t_sq")
                         nc.scalar.activation(
@@ -138,15 +143,12 @@ def tile_netgram_kernel(tc, base, h, rw, offs, out):
                             ACT.Square,
                             accum_out=r[:, blk * O + o : blk * O + o + 1],
                         )
-                    agree = work.tile([P, NETS, N], F32, name="agree")
-                    nc.vector.tensor_mul(agree[:], p[blk][:], t_ps[blk][:].unsqueeze(1).to_broadcast([P, NETS, N]))
-                    if blk == BLOCKS - 1:
-                        nc.scalar.activation(root[:], r[:], ACT.Sqrt)
-                        nc.scalar.activation(denom[:], r[:], ACT.Copy, bias=1.0)
-                        nc.vector.reciprocal(denom[:], denom[:])
                     nc.vector.tensor_reduce(
                         raw[:, blk], agree[:].rearrange("p n (o k) -> p n o k", k=K), axis=AX.X, op=ALU.add
                     )
+                nc.scalar.activation(root[:], r[:], ACT.Sqrt)
+                nc.scalar.activation(denom[:], r[:], ACT.Copy, bias=1.0)
+                nc.vector.reciprocal(denom[:], denom[:])
                 g = small.tile([P, BLOCKS * O], F32, name="g")
                 nc.vector.tensor_mul(g[:], root[:], denom[:])
                 g_for_nets = g[:].rearrange("p (b o) -> p b o", o=O).unsqueeze(2).to_broadcast([P, BLOCKS, NETS, O])

@@ -56,11 +56,18 @@ def tile_netgram_kernel(tc, base, h, rw, offs, out):
         eye_over_o = held.tile([P, P], F32, name="eye_over_o")
         nc.gpsimd.tensor_scalar_mul(eye_over_o[:], eye[:], 1.0 / O)
 
-        def sum_over_nets(blk, terms, weights):
+        def sum_over_nets(terms, count, weights):
             t_ps = sums.tile([P, N], F32, name="t_ps")
-            for n in range(NETS):
-                nc.tensor.matmul(t_ps[:], lhsT=weights[:], rhs=terms[:, n, :], start=(n == 0), stop=(n == NETS - 1))
+            for n in range(count):
+                nc.tensor.matmul(t_ps[:], lhsT=weights[:], rhs=terms[:, n, :], start=(n == 0), stop=(n == count - 1))
             return t_ps
+
+        def folded_twice(terms):
+            four = work.tile([P, NETS // 2, N], F32, name="four")
+            nc.vector.tensor_add(four[:], terms[:, 0 : NETS // 2, :], terms[:, NETS // 2 : NETS, :])
+            two = work.tile([P, NETS // 4, N], F32, name="two")
+            nc.vector.tensor_add(two[:], four[:, 0 : NETS // 4, :], four[:, NETS // 4 : NETS // 2, :])
+            return two
 
         p = []
         for blk in range(BLOCKS):
@@ -99,7 +106,7 @@ def tile_netgram_kernel(tc, base, h, rw, offs, out):
             t_ps = []
             if turn == 0:
                 for blk in range(BLOCKS):
-                    t_ps.append(sum_over_nets(blk, p[blk], eye_over_o))
+                    t_ps.append(sum_over_nets(p[blk], NETS, eye_over_o))
             else:
                 rows = [P, BLOCKS * NETS, O]
                 logit_rows = logit[:].rearrange("p b n o -> p (b n) o")
@@ -114,18 +121,31 @@ def tile_netgram_kernel(tc, base, h, rw, offs, out):
                 nc.vector.tensor_mul(prob[:], prob[:], total[:].unsqueeze(2).to_broadcast(rows))
                 for blk in range(BLOCKS):
                     weighted = per_block.tile([P, NETS, N], F32, name="weighted")
-                    nets_in_piece = 2 if blk == 0 else NETS
-                    for first in range(0, NETS, nets_in_piece):
-                        nets = slice(first, first + nets_in_piece)
-                        nc.vector.tensor_mul(
-                            weighted[:, nets, :].rearrange("p n (o k) -> p (n o) k", k=K),
-                            p[blk][:, nets, :].rearrange("p n (o k) -> p (n o) k", k=K),
-                            prob[:, blk * NETS + first : blk * NETS + first + nets_in_piece, :]
-                            .rearrange("p n o -> p (n o)")
-                            .unsqueeze(2)
-                            .to_broadcast([P, nets_in_piece * O, K]),
-                        )
-                    t_ps.append(sum_over_nets(blk, weighted, eye))
+                    if blk == BLOCKS - 1:
+                        for n in range(NETS):
+                            for o in range(O):
+                                nc.scalar.activation(
+                                    weighted[:, n, o * K : (o + 1) * K],
+                                    p[blk][:, n, o * K : (o + 1) * K],
+                                    ACT.Copy,
+                                    scale=prob[:, blk * NETS + n, o : o + 1],
+                                )
+                    else:
+                        nets_in_piece = 2 if blk == 0 else NETS
+                        for first in range(0, NETS, nets_in_piece):
+                            nets = slice(first, first + nets_in_piece)
+                            nc.vector.tensor_mul(
+                                weighted[:, nets, :].rearrange("p n (o k) -> p (n o) k", k=K),
+                                p[blk][:, nets, :].rearrange("p n (o k) -> p (n o) k", k=K),
+                                prob[:, blk * NETS + first : blk * NETS + first + nets_in_piece, :]
+                                .rearrange("p n o -> p (n o)")
+                                .unsqueeze(2)
+                                .to_broadcast([P, nets_in_piece * O, K]),
+                            )
+                    if blk == BLOCKS - 1:
+                        t_ps.append(sum_over_nets(folded_twice(weighted), NETS // 4, eye))
+                    else:
+                        t_ps.append(sum_over_nets(weighted, NETS, eye))
 
             if turn + 1 < PASSES:
                 r = small.tile([P, BLOCKS * O], F32, name="r")

@@ -11,6 +11,7 @@ AX = mybir.AxisListType
 P = 128
 B, NETS, D, O, K, S, N, PASSES = 512, 8, 128, 8, 32, 2048, 256, 3
 BLOCKS = B // P
+VIA_TENSOR = BLOCKS - 2
 FLOPS = 2 * B * NETS * D * N
 
 
@@ -153,8 +154,12 @@ def tile_netgram_kernel(tc, base, h, rw, offs, out):
                 root = small.tile([P, BLOCKS * O], F32, name="root")
                 denom = small.tile([P, BLOCKS * O], F32, name="denom")
                 for blk in range(BLOCKS):
-                    agree = work.tile([P, NETS, N], F32, name="agree")
-                    nc.vector.tensor_mul(agree[:], p[blk][:], t_ps[blk][:].unsqueeze(1).to_broadcast([P, NETS, N]))
+                    agree = work.tile([P, NETS * O, K], F32, name="agree")
+                    nc.vector.tensor_mul(
+                        agree[:].rearrange("p (n o) k -> p n (o k)", o=O),
+                        p[blk][:],
+                        t_ps[blk][:].unsqueeze(1).to_broadcast([P, NETS, N]),
+                    )
                     for o in range(O):
                         t_sq = small.tile([P, K], F32, name="t_sq")
                         nc.scalar.activation(
@@ -163,9 +168,19 @@ def tile_netgram_kernel(tc, base, h, rw, offs, out):
                             ACT.Square,
                             accum_out=r[:, blk * O + o : blk * O + o + 1],
                         )
-                    nc.vector.tensor_reduce(
-                        raw[:, blk], agree[:].rearrange("p n (o k) -> p n o k", k=K), axis=AX.X, op=ALU.add
-                    )
+                    if blk == VIA_TENSOR:
+                        quarter = votes.tile([P, NETS * O, K // 4], F32, name="votes_ps")
+                        for j in range(4):
+                            nc.tensor.matmul(
+                                quarter[:],
+                                lhsT=eye[:],
+                                rhs=agree[:, :, j * (K // 4) : (j + 1) * (K // 4)],
+                                start=(j == 0),
+                                stop=(j == 3),
+                            )
+                    else:
+                        nc.vector.tensor_reduce(raw[:, blk].rearrange("p n o -> p (n o)"), agree[:], axis=AX.X, op=ALU.add)
+                nc.vector.tensor_reduce(raw[:, VIA_TENSOR].rearrange("p n o -> p (n o)"), quarter[:], axis=AX.X, op=ALU.add)
                 nc.scalar.activation(root[:], r[:], ACT.Sqrt)
                 nc.scalar.activation(denom[:], r[:], ACT.Copy, bias=1.0)
                 nc.vector.reciprocal(denom[:], denom[:])

@@ -11,7 +11,10 @@ AX = mybir.AxisListType
 P = 128
 B, NETS, D, O, K, S, N, PASSES = 512, 8, 128, 8, 32, 2048, 256, 3
 BLOCKS = B // P
-VIA_TENSOR = BLOCKS - 2
+GROUPS = ((0, 1), (2, 3))
+PIECE = NETS // 4
+SPARED = GROUPS[1][0]
+LEFT = 4
 FLOPS = 2 * B * NETS * D * N
 
 
@@ -31,7 +34,7 @@ def tile_netgram_kernel(tc, base, h, rw, offs, out):
     with (
         tc.tile_pool(name="held", bufs=1) as held,
         tc.tile_pool(name="per_block", bufs=BLOCKS) as per_block,
-        tc.tile_pool(name="work", bufs=2) as work,
+        tc.tile_pool(name="work", bufs=3) as work,
         tc.tile_pool(name="small", bufs=2) as small,
         tc.psum_pool(name="flip", bufs=2) as flip,
         tc.psum_pool(name="votes", bufs=2) as votes,
@@ -63,12 +66,13 @@ def tile_netgram_kernel(tc, base, h, rw, offs, out):
                 nc.tensor.matmul(t_ps[:], lhsT=weights[:], rhs=terms[:, n, :], start=(n == 0), stop=(n == count - 1))
             return t_ps
 
-        def folded_twice(terms):
-            four = work.tile([P, NETS // 2, N], F32, name="four")
-            nc.vector.tensor_add(four[:], terms[:, 0 : NETS // 2, :], terms[:, NETS // 2 : NETS, :])
-            two = work.tile([P, NETS // 4, N], F32, name="two")
-            nc.vector.tensor_add(two[:], four[:, 0 : NETS // 4, :], four[:, NETS // 4 : NETS // 2, :])
-            return two
+        def folded(terms, rows):
+            half = work.tile([P, rows // 2, N], F32, name="folded%d" % rows)
+            nc.vector.tensor_add(half[:], terms[:, 0 : rows // 2, :], terms[:, rows // 2 : rows, :])
+            return half
+
+        def by_capsule(rows):
+            return rows.rearrange("p n (o k) -> p (n o) k", k=K)
 
         p = []
         for blk in range(BLOCKS):
@@ -102,107 +106,121 @@ def tile_netgram_kernel(tc, base, h, rw, offs, out):
                         p[blk][:, n, :], votes_ps[:, half * N : (half + 1) * N], ACT.Copy, scale=s[:, n : n + 1]
                     )
 
-        logit = held.tile([P, BLOCKS, NETS, O], F32, name="logit")
-        for turn in range(PASSES):
-            t_ps = []
-            if turn == 0:
-                for blk in range(BLOCKS):
-                    t_ps.append(sum_over_nets(p[blk], NETS, eye_over_o))
-            else:
-                rows = [P, BLOCKS * NETS, O]
-                logit_rows = logit[:].rearrange("p b n o -> p (b n) o")
-                top = small.tile([P, BLOCKS * NETS], F32, name="top")
-                nc.vector.tensor_reduce(top[:], logit_rows, axis=AX.X, op=ALU.max)
-                prob = small.tile(rows, F32, name="prob")
-                nc.vector.tensor_sub(prob[:], logit_rows, top[:].unsqueeze(2).to_broadcast(rows))
-                nc.scalar.activation(prob[:], prob[:], ACT.Exp)
-                total = small.tile([P, BLOCKS * NETS], F32, name="total")
-                nc.vector.tensor_reduce(total[:], prob[:], axis=AX.X, op=ALU.add)
-                nc.vector.reciprocal(total[:], total[:])
-                nc.vector.tensor_mul(prob[:], prob[:], total[:].unsqueeze(2).to_broadcast(rows))
-                for blk in range(BLOCKS):
-                    weighted = per_block.tile([P, NETS, N], F32, name="weighted")
-                    if blk == BLOCKS - 1:
-                        for n in range(NETS):
-                            for o in range(O):
-                                nc.scalar.activation(
-                                    weighted[:, n, o * K : (o + 1) * K],
-                                    p[blk][:, n, o * K : (o + 1) * K],
-                                    ACT.Copy,
-                                    scale=prob[:, blk * NETS + n, o : o + 1],
-                                )
-                    else:
-                        nets_in_piece = 2 if blk == 0 else NETS
-                        for first in range(0, NETS, nets_in_piece):
-                            nets = slice(first, first + nets_in_piece)
-                            nc.vector.tensor_mul(
-                                weighted[:, nets, :].rearrange("p n (o k) -> p (n o) k", k=K),
-                                p[blk][:, nets, :].rearrange("p n (o k) -> p (n o) k", k=K),
-                                prob[:, blk * NETS + first : blk * NETS + first + nets_in_piece, :]
-                                .rearrange("p n o -> p (n o)")
-                                .unsqueeze(2)
-                                .to_broadcast([P, nets_in_piece * O, K]),
-                            )
-                    if blk == BLOCKS - 1:
-                        t_ps.append(sum_over_nets(folded_twice(weighted), NETS // 4, eye))
-                    else:
-                        t_ps.append(sum_over_nets(weighted, NETS, eye))
+        def weighted_votes(blk, prob):
+            weighted = per_block.tile([P, NETS, N], F32, name="weighted")
+            for first in range(0, NETS, PIECE):
+                nets = slice(first, first + PIECE)
+                nc.vector.tensor_mul(
+                    by_capsule(weighted[:, nets, :]),
+                    by_capsule(p[blk][:, nets, :]),
+                    prob[:, nets, :]
+                    .rearrange("p n o -> p (n o)")
+                    .unsqueeze(2)
+                    .to_broadcast([P, PIECE * O, K]),
+                )
+            return weighted
 
-            if turn + 1 < PASSES:
-                r = small.tile([P, BLOCKS * O], F32, name="r")
-                raw = small.tile([P, BLOCKS, NETS, O], F32, name="raw")
-                root = small.tile([P, BLOCKS * O], F32, name="root")
-                denom = small.tile([P, BLOCKS * O], F32, name="denom")
-                for blk in range(BLOCKS):
-                    agree = work.tile([P, NETS * O, K], F32, name="agree")
-                    nc.vector.tensor_mul(
-                        agree[:].rearrange("p (n o) k -> p n (o k)", o=O),
-                        p[blk][:],
-                        t_ps[blk][:].unsqueeze(1).to_broadcast([P, NETS, N]),
-                    )
-                    for o in range(O):
-                        t_sq = small.tile([P, K], F32, name="t_sq")
-                        nc.scalar.activation(
-                            t_sq[:],
-                            t_ps[blk][:, o * K : (o + 1) * K],
-                            ACT.Square,
-                            accum_out=r[:, blk * O + o : blk * O + o + 1],
-                        )
-                    if blk == VIA_TENSOR:
-                        quarter = votes.tile([P, NETS * O, K // 4], F32, name="votes_ps")
-                        for j in range(4):
-                            nc.tensor.matmul(
-                                quarter[:],
-                                lhsT=eye[:],
-                                rhs=agree[:, :, j * (K // 4) : (j + 1) * (K // 4)],
-                                start=(j == 0),
-                                stop=(j == 3),
-                            )
-                    else:
-                        nc.vector.tensor_reduce(raw[:, blk].rearrange("p n o -> p (n o)"), agree[:], axis=AX.X, op=ALU.add)
-                nc.vector.tensor_reduce(raw[:, VIA_TENSOR].rearrange("p n o -> p (n o)"), quarter[:], axis=AX.X, op=ALU.add)
-                nc.scalar.activation(root[:], r[:], ACT.Sqrt)
-                nc.scalar.activation(denom[:], r[:], ACT.Copy, bias=1.0)
-                nc.vector.reciprocal(denom[:], denom[:])
-                g = small.tile([P, BLOCKS * O], F32, name="g")
-                nc.vector.tensor_mul(g[:], root[:], denom[:])
-                g_for_nets = g[:].rearrange("p (b o) -> p b o", o=O).unsqueeze(2).to_broadcast([P, BLOCKS, NETS, O])
-                if turn == 0:
-                    nc.vector.tensor_mul(logit[:], raw[:], g_for_nets)
-                else:
-                    nc.vector.tensor_mul(raw[:], raw[:], g_for_nets)
-                    nc.vector.tensor_add(logit[:], logit[:], raw[:])
-            else:
-                for blk in range(BLOCKS):
-                    t_by_capsule = t_ps[blk][:].rearrange("p (o k) -> p o k", k=K)
-                    last_sq = small.tile([P, O, K], F32, name="last_sq")
-                    nc.scalar.activation(last_sq[:], t_by_capsule, ACT.Square)
-                    last_r = small.tile([P, O], F32, name="last_r")
-                    nc.vector.tensor_reduce(last_r[:], last_sq[:], axis=AX.X, op=ALU.add)
-                    last_g = squash_scale(nc, small, last_r[:], O)
-                    v = small.tile([P, O, K], F32, name="v")
-                    nc.vector.tensor_mul(v[:], t_by_capsule, last_g[:].unsqueeze(2).to_broadcast([P, O, K]))
+        def weighted_votes_on_scalar(blk, prob):
+            weighted = per_block.tile([P, NETS, N], F32, name="weighted")
+            for n in range(NETS):
+                for o in range(O):
+                    capsule = slice(o * K, (o + 1) * K)
                     nc.scalar.activation(
-                        window[blk][:].indirect(offsets[:]), v[:].rearrange("p o k -> p (o k)"), ACT.Copy
+                        weighted[:, n, capsule], p[blk][:, n, capsule], ACT.Copy, scale=prob[:, n, o : o + 1]
                     )
-                    nc.sync.dma_start(out[blk * P : (blk + 1) * P, :], window[blk][:])
+            return weighted
+
+        def agreement(blk, t_ps, raw, r):
+            agree = work.tile([P, NETS * O, K], F32, name="agree")
+            for first in range(0, NETS, PIECE):
+                nc.vector.tensor_mul(
+                    agree[:, first * O : (first + PIECE) * O, :].rearrange("p (n o) k -> p n (o k)", o=O),
+                    p[blk][:, first : first + PIECE, :],
+                    t_ps[:].unsqueeze(1).to_broadcast([P, PIECE, N]),
+                )
+            for o in range(O):
+                t_sq = small.tile([P, K], F32, name="t_sq")
+                nc.scalar.activation(t_sq[:], t_ps[:, o * K : (o + 1) * K], ACT.Square, accum_out=r[:, o : o + 1])
+            if blk == SPARED:
+                part = votes.tile([P, NETS * O, LEFT], F32, name="votes_ps")
+                for k in range(0, K, LEFT):
+                    nc.tensor.matmul(
+                        part[:], lhsT=eye[:], rhs=agree[:, :, k : k + LEFT], start=(k == 0), stop=(k + LEFT == K)
+                    )
+                nc.vector.tensor_reduce(raw, part[:], axis=AX.X, op=ALU.add)
+                return
+            for first in range(0, NETS * O, PIECE * O):
+                rows = slice(first, first + PIECE * O)
+                nc.vector.tensor_reduce(raw[:, rows], agree[:, rows, :], axis=AX.X, op=ALU.add)
+
+        def new_probabilities(group, turn, raw, r):
+            blocks = len(GROUPS[group])
+            root = small.tile([P, blocks * O], F32, name="root_of_r")
+            nc.scalar.activation(root[:], r[:], ACT.Sqrt)
+            denom = small.tile([P, blocks * O], F32, name="denom_of_r")
+            nc.scalar.activation(denom[:], r[:], ACT.Copy, bias=1.0)
+            nc.vector.reciprocal(denom[:], denom[:])
+            g = small.tile([P, blocks * O], F32, name="g")
+            nc.vector.tensor_mul(g[:], root[:], denom[:])
+            g_for_nets = g[:].rearrange("p (b o) -> p b o", o=O).unsqueeze(2).to_broadcast([P, blocks, NETS, O])
+            raw_rows = raw[:].rearrange("p b (n o) -> p b n o", o=O)
+            if turn == 0:
+                nc.vector.tensor_mul(logit[group][:], raw_rows, g_for_nets)
+            else:
+                nc.vector.tensor_mul(raw_rows, raw_rows, g_for_nets)
+                nc.vector.tensor_add(logit[group][:], logit[group][:], raw_rows)
+
+            rows = [P, blocks * NETS, O]
+            logit_rows = logit[group][:].rearrange("p b n o -> p (b n) o")
+            top = small.tile([P, blocks * NETS], F32, name="top")
+            nc.vector.tensor_reduce(top[:], logit_rows, axis=AX.X, op=ALU.max)
+            prob = small.tile(rows, F32, name="prob")
+            nc.vector.tensor_sub(prob[:], logit_rows, top[:].unsqueeze(2).to_broadcast(rows))
+            nc.scalar.activation(prob[:], prob[:], ACT.Exp)
+            total = small.tile([P, blocks * NETS], F32, name="total")
+            nc.vector.tensor_reduce(total[:], prob[:], axis=AX.X, op=ALU.add)
+            nc.vector.reciprocal(total[:], total[:])
+            nc.vector.tensor_mul(prob[:], prob[:], total[:].unsqueeze(2).to_broadcast(rows))
+            return prob
+
+        def finish(blk, t_ps):
+            t_by_capsule = t_ps[:].rearrange("p (o k) -> p o k", k=K)
+            last_sq = small.tile([P, O, K], F32, name="last_sq")
+            nc.scalar.activation(last_sq[:], t_by_capsule, ACT.Square)
+            last_r = small.tile([P, O], F32, name="last_r")
+            nc.vector.tensor_reduce(last_r[:], last_sq[:], axis=AX.X, op=ALU.add)
+            last_g = squash_scale(nc, small, last_r[:], O)
+            v = small.tile([P, O, K], F32, name="v")
+            nc.vector.tensor_mul(v[:], t_by_capsule, last_g[:].unsqueeze(2).to_broadcast([P, O, K]))
+            nc.scalar.activation(window[blk][:].indirect(offsets[:]), v[:].rearrange("p o k -> p (o k)"), ACT.Copy)
+            nc.sync.dma_start(out[blk * P : (blk + 1) * P, :], window[blk][:])
+
+        logit = [held.tile([P, len(blocks), NETS, O], F32, name="logit%d" % i) for i, blocks in enumerate(GROUPS)]
+        prob = [None, None]
+        for turn in range(PASSES):
+            for group, blocks in enumerate(GROUPS):
+                t_ps = []
+                for i, blk in enumerate(blocks):
+                    if turn == 0:
+                        terms, count = p[blk], NETS
+                        if blk == 0:
+                            terms, count = folded(folded(terms, NETS), NETS // 2), NETS // 4
+                        t_ps.append(sum_over_nets(terms, count, eye_over_o))
+                        continue
+                    block_prob = prob[group][:, i * NETS : (i + 1) * NETS, :]
+                    if turn == 1 and blk == SPARED:
+                        terms, count = weighted_votes_on_scalar(blk, block_prob), NETS
+                    else:
+                        terms, count = weighted_votes(blk, block_prob), NETS
+                    if turn == PASSES - 1 and group == 1:
+                        terms, count = folded(terms, NETS), NETS // 2
+                    t_ps.append(sum_over_nets(terms, count, eye))
+                if turn + 1 < PASSES:
+                    raw = small.tile([P, len(blocks), NETS * O], F32, name="raw")
+                    r = small.tile([P, len(blocks) * O], F32, name="r")
+                    for i, blk in enumerate(blocks):
+                        agreement(blk, t_ps[i], raw[:, i, :], r[:, i * O : (i + 1) * O])
+                    prob[group] = new_probabilities(group, turn, raw, r)
+                else:
+                    for i, blk in enumerate(blocks):
+                        finish(blk, t_ps[i])

@@ -40,18 +40,23 @@ def tile_netgram_kernel(tc, base, h, rw, offs, out):
         tc.psum_pool(name="votes", bufs=2) as votes,
         tc.psum_pool(name="sums", bufs=BLOCKS) as sums,
     ):
-        h_sb = []
-        for blk in range(BLOCKS):
-            h_sb.append(per_block.tile([P, NETS * D], BF16, name="h_sb"))
-            nc.sync.dma_start(h_sb[blk][:], h[blk * P : (blk + 1) * P, :])
         rw_sb = held.tile([P, NETS, N], BF16, name="rw_sb")
         nc.scalar.dma_start(rw_sb[:], rw.rearrange("n d m -> d n m"))
         offsets = held.tile([P, N // 16], U16, name="offsets")
-        nc.sync.dma_start(offsets[:], offs)
-        window = []
-        for blk in range(BLOCKS):
-            window.append(per_block.tile([P, S], F32, name="window"))
-            nc.sync.dma_start(window[blk][:], base[blk * P : (blk + 1) * P, :])
+        h_sb, window = [], []
+        for blocks in GROUPS:
+            for blk in blocks:
+                h_sb.append(per_block.tile([P, NETS * D], BF16, name="h_sb"))
+                nc.sync.dma_start(h_sb[blk][:], h[blk * P : (blk + 1) * P, :])
+            if blocks == GROUPS[0]:
+                nc.sync.dma_start(offsets[:], offs)
+            for blk in blocks:
+                window.append(per_block.tile([P, S], F32, name="window"))
+                nc.sync.dma_start(window[blk][:], base[blk * P : (blk + 1) * P, :])
+
+        one = held.tile([P, 1], F32, name="one")
+        nc.vector.memset(one[:], 1.0)
+        nc.scalar.activation(one[:], one[:], ACT.Sqrt)
 
         identity = held.tile([P, P], BF16, name="identity")
         make_identity(nc, identity[:])
@@ -77,34 +82,37 @@ def tile_netgram_kernel(tc, base, h, rw, offs, out):
         p = []
         for blk in range(BLOCKS):
             q = small.tile([P, NETS], F32, name="q")
-            squares = small.tile([P, D], F32, name="squares")
+            squares = small.tile([P, NETS * D], F32, name="squares")
             for n in range(NETS):
                 nc.scalar.activation(
-                    squares[:], h_sb[blk][:, n * D : (n + 1) * D], ACT.Square, accum_out=q[:, n : n + 1]
+                    squares[:, n * D : (n + 1) * D],
+                    h_sb[blk][:, n * D : (n + 1) * D],
+                    ACT.Square,
+                    accum_out=q[:, n : n + 1],
                 )
             s = squash_scale(nc, small, q[:], NETS)
 
-            hT_ps = flip.tile([P, NETS * P], BF16, name="hT_ps")
-            for n in range(NETS):
-                nc.tensor.transpose(hT_ps[:, n * P : (n + 1) * P], h_sb[blk][:, n * D : (n + 1) * D], identity[:])
             hT = per_block.tile([P, NETS * P], BF16, name="hT")
-            nc.vector.tensor_copy(hT[:], hT_ps[:])
+            for pair in range(NETS // 2):
+                hT_ps = flip.tile([P, 2 * P], BF16, name="hT_ps")
+                for half in range(2):
+                    n = 2 * pair + half
+                    nc.tensor.transpose(
+                        hT_ps[:, half * P : (half + 1) * P], h_sb[blk][:, n * D : (n + 1) * D], identity[:]
+                    )
+                nc.vector.tensor_copy(hT[:, 2 * pair * P : (2 * pair + 2) * P], hT_ps[:])
 
             p.append(per_block.tile([P, NETS, N], F32, name="p"))
             for pair in range(NETS // 2):
-                votes_ps = votes.tile([P, 2 * N], F32, name="votes_ps")
+                votes_ps = votes.tile([P, 2, N], F32, name="votes_ps")
                 for half in range(2):
                     n = 2 * pair + half
                     nc.tensor.matmul(
-                        votes_ps[:, half * N : (half + 1) * N],
-                        lhsT=hT[:, n * P : (n + 1) * P],
-                        rhs=rw_sb[:, n, :],
-                        start=True,
-                        stop=True,
+                        votes_ps[:, half, :], lhsT=hT[:, n * P : (n + 1) * P], rhs=rw_sb[:, n, :], start=True, stop=True
                     )
-                    nc.scalar.activation(
-                        p[blk][:, n, :], votes_ps[:, half * N : (half + 1) * N], ACT.Copy, scale=s[:, n : n + 1]
-                    )
+                for half in range(2):
+                    n = 2 * pair + half
+                    nc.scalar.activation(p[blk][:, n, :], votes_ps[:, half, :], ACT.Copy, scale=s[:, n : n + 1])
 
         def weighted_votes(blk, prob):
             weighted = per_block.tile([P, NETS, N], F32, name="weighted")
@@ -138,9 +146,10 @@ def tile_netgram_kernel(tc, base, h, rw, offs, out):
                     p[blk][:, first : first + PIECE, :],
                     t_ps[:].unsqueeze(1).to_broadcast([P, PIECE, N]),
                 )
+            t_sq = small.tile([P, N], F32, name="t_sq")
             for o in range(O):
-                t_sq = small.tile([P, K], F32, name="t_sq")
-                nc.scalar.activation(t_sq[:], t_ps[:, o * K : (o + 1) * K], ACT.Square, accum_out=r[:, o : o + 1])
+                capsule = slice(o * K, (o + 1) * K)
+                nc.scalar.activation(t_sq[:, capsule], t_ps[:, capsule], ACT.Square, accum_out=r[:, o : o + 1])
             if blk == SPARED:
                 part = votes.tile([P, NETS * O, LEFT], F32, name="votes_ps")
                 for k in range(0, K, LEFT):
@@ -203,7 +212,7 @@ def tile_netgram_kernel(tc, base, h, rw, offs, out):
                 for i, blk in enumerate(blocks):
                     if turn == 0:
                         terms, count = p[blk], NETS
-                        if blk == 0:
+                        if group == 0:
                             terms, count = folded(folded(terms, NETS), NETS // 2), NETS // 4
                         t_ps.append(sum_over_nets(terms, count, eye_over_o))
                         continue

@@ -1,5 +1,4 @@
 import concourse.mybir as mybir
-from concourse.masks import make_identity
 
 F32 = mybir.dt.float32
 BF16 = mybir.dt.bfloat16
@@ -11,6 +10,7 @@ AX = mybir.AxisListType
 P = 128
 B, NETS, D, O, K, S, N, PASSES = 512, 8, 128, 8, 32, 2048, 256, 3
 BLOCKS = B // P
+SQUARE = 32
 GROUPS = ((0, 1), (2, 3))
 PIECE = NETS // 4
 SPARED = GROUPS[1][0]
@@ -58,12 +58,23 @@ def tile_netgram_kernel(tc, base, h, rw, offs, out):
         nc.vector.memset(one[:], 1.0)
         nc.scalar.activation(one[:], one[:], ACT.Sqrt)
 
-        identity = held.tile([P, P], BF16, name="identity")
-        make_identity(nc, identity[:])
+        count = held.tile([P, SQUARE], F32, name="count", align_bytes=64)
+        nc.vector.memset(count[:, 0:1], 0.0)
+        width = 1
+        while width < SQUARE:
+            nc.vector.tensor_scalar_add(count[:, width : 2 * width], count[:, 0:width], float(width))
+            width = 2 * width
+        flipped = held.tile([P, SQUARE], F32, name="flipped", align_bytes=64)
+        nc.vector.transpose(flipped[:], count[:])
         eye = held.tile([P, P], F32, name="eye")
-        make_identity(nc, eye[:])
+        nc.vector.memset(eye[:], 0.0)
+        for first in range(0, P, SQUARE):
+            rows = slice(first, first + SQUARE)
+            nc.vector.tensor_tensor(eye[rows, rows], flipped[rows, :], count[rows, :], ALU.is_equal)
+        identity = held.tile([P, P], BF16, name="identity")
+        nc.vector.tensor_copy(identity[:], eye[:])
         eye_over_o = held.tile([P, P], F32, name="eye_over_o")
-        nc.gpsimd.tensor_scalar_mul(eye_over_o[:], eye[:], 1.0 / O)
+        nc.vector.tensor_scalar_mul(eye_over_o[:], eye[:], 1.0 / O)
 
         def sum_over_nets(terms, count, weights):
             t_ps = sums.tile([P, N], F32, name="t_ps")
@@ -114,23 +125,16 @@ def tile_netgram_kernel(tc, base, h, rw, offs, out):
                     n = 2 * pair + half
                     nc.scalar.activation(p[blk][:, n, :], votes_ps[:, half, :], ACT.Copy, scale=s[:, n : n + 1])
 
-        def weighted_votes(blk, prob):
+        def weighted_votes(blk, prob, by_vector):
             weighted = per_block.tile([P, NETS, N], F32, name="weighted")
-            for first in range(0, NETS, PIECE):
+            for first in range(0, by_vector, PIECE):
                 nets = slice(first, first + PIECE)
                 nc.vector.tensor_mul(
                     by_capsule(weighted[:, nets, :]),
                     by_capsule(p[blk][:, nets, :]),
-                    prob[:, nets, :]
-                    .rearrange("p n o -> p (n o)")
-                    .unsqueeze(2)
-                    .to_broadcast([P, PIECE * O, K]),
+                    prob[:, nets, :].rearrange("p n o -> p (n o)").unsqueeze(2).to_broadcast([P, PIECE * O, K]),
                 )
-            return weighted
-
-        def weighted_votes_on_scalar(blk, prob):
-            weighted = per_block.tile([P, NETS, N], F32, name="weighted")
-            for n in range(NETS):
+            for n in range(by_vector, NETS):
                 for o in range(O):
                     capsule = slice(o * K, (o + 1) * K)
                     nc.scalar.activation(
@@ -195,7 +199,12 @@ def tile_netgram_kernel(tc, base, h, rw, offs, out):
         def finish(blk, t_ps):
             t_by_capsule = t_ps[:].rearrange("p (o k) -> p o k", k=K)
             last_sq = small.tile([P, O, K], F32, name="last_sq")
-            nc.scalar.activation(last_sq[:], t_by_capsule, ACT.Square)
+            if blk == BLOCKS - 1:
+                t_sb = small.tile([P, O, K], F32, name="t_sb")
+                nc.vector.tensor_copy(t_sb[:], t_by_capsule)
+                nc.vector.tensor_mul(last_sq[:], t_by_capsule, t_sb[:])
+            else:
+                nc.scalar.activation(last_sq[:], t_by_capsule, ACT.Square)
             last_r = small.tile([P, O], F32, name="last_r")
             nc.vector.tensor_reduce(last_r[:], last_sq[:], axis=AX.X, op=ALU.add)
             last_g = squash_scale(nc, small, last_r[:], O)
@@ -218,9 +227,12 @@ def tile_netgram_kernel(tc, base, h, rw, offs, out):
                         continue
                     block_prob = prob[group][:, i * NETS : (i + 1) * NETS, :]
                     if turn == 1 and blk == SPARED:
-                        terms, count = weighted_votes_on_scalar(blk, block_prob), NETS
+                        by_vector = 0
+                    elif turn == PASSES - 1 and blk == BLOCKS - 1:
+                        by_vector = NETS // 2
                     else:
-                        terms, count = weighted_votes(blk, block_prob), NETS
+                        by_vector = NETS
+                    terms, count = weighted_votes(blk, block_prob, by_vector), NETS
                     if turn == PASSES - 1 and group == 1:
                         terms, count = folded(terms, NETS), NETS // 2
                     t_ps.append(sum_over_nets(terms, count, eye))

@@ -82,9 +82,14 @@ def tile_netgram_kernel(tc, base, h, rw, offs, out):
                 nc.tensor.matmul(t_ps[:], lhsT=weights[:], rhs=terms[:, n, :], start=(n == 0), stop=(n == count - 1))
             return t_ps
 
-        def folded(terms, rows):
-            half = work.tile([P, rows // 2, N], F32, name="folded%d" % rows)
-            nc.vector.tensor_add(half[:], terms[:, 0 : rows // 2, :], terms[:, rows // 2 : rows, :])
+        def folded(terms, rows, pieces):
+            left = rows // 2
+            half = work.tile([P, left, N], F32, name="folded%d" % rows)
+            piece = left // pieces
+            for first in range(0, left, piece):
+                lower = slice(first, first + piece)
+                upper = slice(left + first, left + first + piece)
+                nc.vector.tensor_add(half[:, lower, :], terms[:, lower, :], terms[:, upper, :])
             return half
 
         def by_capsule(rows):
@@ -115,12 +120,18 @@ def tile_netgram_kernel(tc, base, h, rw, offs, out):
 
             p.append(per_block.tile([P, NETS, N], F32, name="p"))
             for pair in range(NETS // 2):
+                nets = slice(2 * pair, 2 * pair + 2)
                 votes_ps = votes.tile([P, 2, N], F32, name="votes_ps")
                 for half in range(2):
                     n = 2 * pair + half
                     nc.tensor.matmul(
                         votes_ps[:, half, :], lhsT=hT[:, n * P : (n + 1) * P], rhs=rw_sb[:, n, :], start=True, stop=True
                     )
+                if blk == 0:
+                    nc.vector.tensor_mul(
+                        p[blk][:, nets, :], votes_ps[:], s[:, nets].unsqueeze(2).to_broadcast([P, 2, N])
+                    )
+                    continue
                 for half in range(2):
                     n = 2 * pair + half
                     nc.scalar.activation(p[blk][:, n, :], votes_ps[:, half, :], ACT.Copy, scale=s[:, n : n + 1])
@@ -148,7 +159,7 @@ def tile_netgram_kernel(tc, base, h, rw, offs, out):
                 nc.vector.tensor_mul(
                     agree[:, first * O : (first + PIECE) * O, :].rearrange("p (n o) k -> p n (o k)", o=O),
                     p[blk][:, first : first + PIECE, :],
-                    t_ps[:].unsqueeze(1).to_broadcast([P, PIECE, N]),
+                    t_ps.unsqueeze(1).to_broadcast([P, PIECE, N]),
                 )
             t_sq = small.tile([P, N], F32, name="t_sq")
             for o in range(O):
@@ -197,12 +208,10 @@ def tile_netgram_kernel(tc, base, h, rw, offs, out):
             return prob
 
         def finish(blk, t_ps):
-            t_by_capsule = t_ps[:].rearrange("p (o k) -> p o k", k=K)
+            t_by_capsule = t_ps.rearrange("p (o k) -> p o k", k=K)
             last_sq = small.tile([P, O, K], F32, name="last_sq")
             if blk == BLOCKS - 1:
-                t_sb = small.tile([P, O, K], F32, name="t_sb")
-                nc.vector.tensor_copy(t_sb[:], t_by_capsule)
-                nc.vector.tensor_mul(last_sq[:], t_by_capsule, t_sb[:])
+                nc.vector.tensor_mul(last_sq[:], t_by_capsule, t_by_capsule)
             else:
                 nc.scalar.activation(last_sq[:], t_by_capsule, ACT.Square)
             last_r = small.tile([P, O], F32, name="last_r")
@@ -222,8 +231,8 @@ def tile_netgram_kernel(tc, base, h, rw, offs, out):
                     if turn == 0:
                         terms, count = p[blk], NETS
                         if group == 0:
-                            terms, count = folded(folded(terms, NETS), NETS // 2), NETS // 4
-                        t_ps.append(sum_over_nets(terms, count, eye_over_o))
+                            terms, count = folded(folded(terms, NETS, 2), NETS // 2, 2), NETS // 4
+                        t_ps.append(sum_over_nets(terms, count, eye_over_o)[:])
                         continue
                     block_prob = prob[group][:, i * NETS : (i + 1) * NETS, :]
                     if turn == 1 and blk == SPARED:
@@ -233,9 +242,14 @@ def tile_netgram_kernel(tc, base, h, rw, offs, out):
                     else:
                         by_vector = NETS
                     terms, count = weighted_votes(blk, block_prob, by_vector), NETS
+                    if turn == PASSES - 1 and blk == BLOCKS - 1:
+                        for rows in (8, 4, 2):
+                            terms = folded(terms, rows, 1)
+                        t_ps.append(terms[:, 0, :])
+                        continue
                     if turn == PASSES - 1 and group == 1:
-                        terms, count = folded(terms, NETS), NETS // 2
-                    t_ps.append(sum_over_nets(terms, count, eye))
+                        terms, count = folded(terms, NETS, 1), NETS // 2
+                    t_ps.append(sum_over_nets(terms, count, eye)[:])
                 if turn + 1 < PASSES:
                     raw = small.tile([P, len(blocks), NETS * O], F32, name="raw")
                     r = small.tile([P, len(blocks) * O], F32, name="r")

@@ -74,7 +74,7 @@ def tile_netgram_kernel(tc, base, h, rw, offs, out):
         identity = held.tile([P, P], BF16, name="identity")
         nc.vector.tensor_copy(identity[:], eye[:])
         eye_over_o = held.tile([P, P], F32, name="eye_over_o")
-        nc.vector.tensor_scalar_mul(eye_over_o[:], eye[:], 1.0 / O)
+        nc.gpsimd.tensor_scalar_mul(eye_over_o[:], eye[:], 1.0 / O)
 
         def sum_over_nets(terms, count, weights):
             t_ps = sums.tile([P, N], F32, name="t_ps")
@@ -175,7 +175,12 @@ def tile_netgram_kernel(tc, base, h, rw, offs, out):
                 return
             for first in range(0, NETS * O, PIECE * O):
                 rows = slice(first, first + PIECE * O)
-                nc.vector.tensor_reduce(raw[:, rows], agree[:, rows, :], axis=AX.X, op=ALU.add)
+                if blk == BLOCKS - 1:
+                    half_sum = work.tile([P, PIECE * O, K // 2], F32, name="half_sum")
+                    nc.gpsimd.tensor_add(half_sum[:], agree[:, rows, 0 : K // 2], agree[:, rows, K // 2 : K])
+                    nc.vector.tensor_reduce(raw[:, rows], half_sum[:], axis=AX.X, op=ALU.add)
+                else:
+                    nc.vector.tensor_reduce(raw[:, rows], agree[:, rows, :], axis=AX.X, op=ALU.add)
 
         def new_probabilities(group, turn, raw, r):
             blocks = len(GROUPS[group])
@@ -183,6 +188,8 @@ def tile_netgram_kernel(tc, base, h, rw, offs, out):
             nc.scalar.activation(root[:], r[:], ACT.Sqrt)
             denom = small.tile([P, blocks * O], F32, name="denom_of_r")
             nc.scalar.activation(denom[:], r[:], ACT.Copy, bias=1.0)
+            warm = small.tile([P, 1], F32, name="warm")
+            nc.scalar.activation(warm[:], root[:, 0:1], ACT.Exp, scale=0.0)
             nc.vector.reciprocal(denom[:], denom[:])
             g = small.tile([P, blocks * O], F32, name="g")
             nc.vector.tensor_mul(g[:], root[:], denom[:])
@@ -201,6 +208,7 @@ def tile_netgram_kernel(tc, base, h, rw, offs, out):
             prob = small.tile(rows, F32, name="prob")
             nc.vector.tensor_sub(prob[:], logit_rows, top[:].unsqueeze(2).to_broadcast(rows))
             nc.scalar.activation(prob[:], prob[:], ACT.Exp)
+            nc.scalar.activation(warm[:], prob[:, 0, 0:1], ACT.Sqrt)
             total = small.tile([P, blocks * NETS], F32, name="total")
             nc.vector.tensor_reduce(total[:], prob[:], axis=AX.X, op=ALU.add)
             nc.vector.reciprocal(total[:], total[:])

@@ -175,7 +175,7 @@ def tile_netgram_kernel(tc, base, h, rw, offs, out):
                 return
             for first in range(0, NETS * O, PIECE * O):
                 rows = slice(first, first + PIECE * O)
-                if blk == BLOCKS - 1:
+                if first % (2 * PIECE * O) == 0:
                     half_sum = work.tile([P, PIECE * O, K // 2], F32, name="half_sum")
                     nc.gpsimd.tensor_add(half_sum[:], agree[:, rows, 0 : K // 2], agree[:, rows, K // 2 : K])
                     nc.vector.tensor_reduce(raw[:, rows], half_sum[:], axis=AX.X, op=ALU.add)

@@ -252,11 +252,11 @@ def tile_netgram_kernel(tc, base, h, rw, offs, out):
                     terms, count = weighted_votes(blk, block_prob, by_vector), NETS
                     if turn == PASSES - 1 and blk == BLOCKS - 1:
                         for rows in (8, 4, 2):
-                            terms = folded(terms, rows, 1)
+                            terms = folded(terms, rows, 2 if rows > 2 else 1)
                         t_ps.append(terms[:, 0, :])
                         continue
                     if turn == PASSES - 1 and group == 1:
-                        terms, count = folded(terms, NETS, 1), NETS // 2
+                        terms, count = folded(terms, NETS, 2), NETS // 2
                     t_ps.append(sum_over_nets(terms, count, eye)[:])
                 if turn + 1 < PASSES:
                     raw = small.tile([P, len(blocks), NETS * O], F32, name="raw")

@@ -127,7 +127,7 @@ def tile_netgram_kernel(tc, base, h, rw, offs, out):
                     nc.tensor.matmul(
                         votes_ps[:, half, :], lhsT=hT[:, n * P : (n + 1) * P], rhs=rw_sb[:, n, :], start=True, stop=True
                     )
-                if blk == 0:
+                if blk == 0 and pair % 2 == 1:
                     nc.vector.tensor_mul(
                         p[blk][:, nets, :], votes_ps[:], s[:, nets].unsqueeze(2).to_broadcast([P, 2, N])
                     )

import concourse.mybir as mybir

F32 = mybir.dt.float32
BF16 = mybir.dt.bfloat16
U16 = mybir.dt.uint16
ACT = mybir.ActivationFunctionType
ALU = mybir.AluOpType
AX = mybir.AxisListType

P = 128
B, NETS, D, O, K, S, N, PASSES = 512, 8, 128, 8, 32, 2048, 256, 3
BLOCKS = B // P
SQUARE = 32
GROUPS = ((0, 1), (2, 3))
PIECE = NETS // 4
SPARED = GROUPS[1][0]
LEFT = 4
FLOPS = 2 * B * NETS * D * N


def squash_scale(nc, pool, sq_norm, width):
    root = pool.tile([P, width], F32, name="root")
    nc.scalar.activation(root[:], sq_norm, ACT.Sqrt)
    denom = pool.tile([P, width], F32, name="denom")
    nc.vector.tensor_scalar_add(denom[:], sq_norm, 1.0)
    nc.vector.reciprocal(denom[:], denom[:])
    scale = pool.tile([P, width], F32, name="scale")
    nc.vector.tensor_mul(scale[:], root[:], denom[:])
    return scale


def tile_netgram_kernel(tc, base, h, rw, offs, out):
    nc = tc.nc
    with (
        tc.tile_pool(name="held", bufs=1) as held,
        tc.tile_pool(name="per_block", bufs=BLOCKS) as per_block,
        tc.tile_pool(name="work", bufs=3) as work,
        tc.tile_pool(name="small", bufs=2) as small,
        tc.psum_pool(name="flip", bufs=2) as flip,
        tc.psum_pool(name="votes", bufs=2) as votes,
        tc.psum_pool(name="sums", bufs=BLOCKS) as sums,
    ):
        rw_sb = held.tile([P, NETS, N], BF16, name="rw_sb")
        nc.scalar.dma_start(rw_sb[:], rw.rearrange("n d m -> d n m"))
        offsets = held.tile([P, N // 16], U16, name="offsets")
        h_sb, window = [], []
        for blocks in GROUPS:
            for blk in blocks:
                h_sb.append(per_block.tile([P, NETS * D], BF16, name="h_sb"))
                nc.sync.dma_start(h_sb[blk][:], h[blk * P : (blk + 1) * P, :])
            if blocks == GROUPS[0]:
                nc.sync.dma_start(offsets[:], offs)
            for blk in blocks:
                window.append(per_block.tile([P, S], F32, name="window"))
                nc.sync.dma_start(window[blk][:], base[blk * P : (blk + 1) * P, :])

        one = held.tile([P, 1], F32, name="one")
        nc.vector.memset(one[:], 1.0)
        nc.scalar.activation(one[:], one[:], ACT.Sqrt)

        count = held.tile([P, SQUARE], F32, name="count", align_bytes=64)
        nc.vector.memset(count[:, 0:1], 0.0)
        width = 1
        while width < SQUARE:
            nc.vector.tensor_scalar_add(count[:, width : 2 * width], count[:, 0:width], float(width))
            width = 2 * width
        flipped = held.tile([P, SQUARE], F32, name="flipped", align_bytes=64)
        nc.vector.transpose(flipped[:], count[:])
        eye = held.tile([P, P], F32, name="eye")
        nc.vector.memset(eye[:], 0.0)
        for first in range(0, P, SQUARE):
            rows = slice(first, first + SQUARE)
            nc.vector.tensor_tensor(eye[rows, rows], flipped[rows, :], count[rows, :], ALU.is_equal)
        identity = held.tile([P, P], BF16, name="identity")
        nc.vector.tensor_copy(identity[:], eye[:])
        eye_over_o = held.tile([P, P], F32, name="eye_over_o")
        nc.gpsimd.tensor_scalar_mul(eye_over_o[:], eye[:], 1.0 / O)

        def sum_over_nets(terms, count, weights):
            t_ps = sums.tile([P, N], F32, name="t_ps")
            for n in range(count):
                nc.tensor.matmul(t_ps[:], lhsT=weights[:], rhs=terms[:, n, :], start=(n == 0), stop=(n == count - 1))
            return t_ps

        def folded(terms, rows, pieces):
            left = rows // 2
            half = work.tile([P, left, N], F32, name="folded%d" % rows)
            piece = left // pieces
            for first in range(0, left, piece):
                lower = slice(first, first + piece)
                upper = slice(left + first, left + first + piece)
                nc.vector.tensor_add(half[:, lower, :], terms[:, lower, :], terms[:, upper, :])
            return half

        def by_capsule(rows):
            return rows.rearrange("p n (o k) -> p (n o) k", k=K)

        p = []
        for blk in range(BLOCKS):
            q = small.tile([P, NETS], F32, name="q")
            squares = small.tile([P, NETS * D], F32, name="squares")
            for n in range(NETS):
                nc.scalar.activation(
                    squares[:, n * D : (n + 1) * D],
                    h_sb[blk][:, n * D : (n + 1) * D],
                    ACT.Square,
                    accum_out=q[:, n : n + 1],
                )
            s = squash_scale(nc, small, q[:], NETS)

            hT = per_block.tile([P, NETS * P], BF16, name="hT")
            for pair in range(NETS // 2):
                hT_ps = flip.tile([P, 2 * P], BF16, name="hT_ps")
                for half in range(2):
                    n = 2 * pair + half
                    nc.tensor.transpose(
                        hT_ps[:, half * P : (half + 1) * P], h_sb[blk][:, n * D : (n + 1) * D], identity[:]
                    )
                nc.vector.tensor_copy(hT[:, 2 * pair * P : (2 * pair + 2) * P], hT_ps[:])

            p.append(per_block.tile([P, NETS, N], F32, name="p"))
            for pair in range(NETS // 2):
                nets = slice(2 * pair, 2 * pair + 2)
                votes_ps = votes.tile([P, 2, N], F32, name="votes_ps")
                for half in range(2):
                    n = 2 * pair + half
                    nc.tensor.matmul(
                        votes_ps[:, half, :], lhsT=hT[:, n * P : (n + 1) * P], rhs=rw_sb[:, n, :], start=True, stop=True
                    )
                if blk == 0 and pair % 2 == 1:
                    nc.vector.tensor_mul(
                        p[blk][:, nets, :], votes_ps[:], s[:, nets].unsqueeze(2).to_broadcast([P, 2, N])
                    )
                    continue
                for half in range(2):
                    n = 2 * pair + half
                    nc.scalar.activation(p[blk][:, n, :], votes_ps[:, half, :], ACT.Copy, scale=s[:, n : n + 1])

        def weighted_votes(blk, prob, by_vector):
            weighted = per_block.tile([P, NETS, N], F32, name="weighted")
            for first in range(0, by_vector, PIECE):
                nets = slice(first, first + PIECE)
                nc.vector.tensor_mul(
                    by_capsule(weighted[:, nets, :]),
                    by_capsule(p[blk][:, nets, :]),
                    prob[:, nets, :].rearrange("p n o -> p (n o)").unsqueeze(2).to_broadcast([P, PIECE * O, K]),
                )
            for n in range(by_vector, NETS):
                for o in range(O):
                    capsule = slice(o * K, (o + 1) * K)
                    nc.scalar.activation(
                        weighted[:, n, capsule], p[blk][:, n, capsule], ACT.Copy, scale=prob[:, n, o : o + 1]
                    )
            return weighted

        def agreement(blk, t_ps, raw, r):
            agree = work.tile([P, NETS * O, K], F32, name="agree")
            for first in range(0, NETS, PIECE):
                nc.vector.tensor_mul(
                    agree[:, first * O : (first + PIECE) * O, :].rearrange("p (n o) k -> p n (o k)", o=O),
                    p[blk][:, first : first + PIECE, :],
                    t_ps.unsqueeze(1).to_broadcast([P, PIECE, N]),
                )
            t_sq = small.tile([P, N], F32, name="t_sq")
            for o in range(O):
                capsule = slice(o * K, (o + 1) * K)
                nc.scalar.activation(t_sq[:, capsule], t_ps[:, capsule], ACT.Square, accum_out=r[:, o : o + 1])
            if blk == SPARED:
                part = votes.tile([P, NETS * O, LEFT], F32, name="votes_ps")
                for k in range(0, K, LEFT):
                    nc.tensor.matmul(
                        part[:], lhsT=eye[:], rhs=agree[:, :, k : k + LEFT], start=(k == 0), stop=(k + LEFT == K)
                    )
                nc.vector.tensor_reduce(raw, part[:], axis=AX.X, op=ALU.add)
                return
            for first in range(0, NETS * O, PIECE * O):
                rows = slice(first, first + PIECE * O)
                if first % (2 * PIECE * O) == 0:
                    half_sum = work.tile([P, PIECE * O, K // 2], F32, name="half_sum")
                    nc.gpsimd.tensor_add(half_sum[:], agree[:, rows, 0 : K // 2], agree[:, rows, K // 2 : K])
                    nc.vector.tensor_reduce(raw[:, rows], half_sum[:], axis=AX.X, op=ALU.add)
                else:
                    nc.vector.tensor_reduce(raw[:, rows], agree[:, rows, :], axis=AX.X, op=ALU.add)

        def new_probabilities(group, turn, raw, r):
            blocks = len(GROUPS[group])
            root = small.tile([P, blocks * O], F32, name="root_of_r")
            nc.scalar.activation(root[:], r[:], ACT.Sqrt)
            denom = small.tile([P, blocks * O], F32, name="denom_of_r")
            nc.scalar.activation(denom[:], r[:], ACT.Copy, bias=1.0)
            warm = small.tile([P, 1], F32, name="warm")
            nc.scalar.activation(warm[:], root[:, 0:1], ACT.Exp, scale=0.0)
            nc.vector.reciprocal(denom[:], denom[:])
            g = small.tile([P, blocks * O], F32, name="g")
            nc.vector.tensor_mul(g[:], root[:], denom[:])
            g_for_nets = g[:].rearrange("p (b o) -> p b o", o=O).unsqueeze(2).to_broadcast([P, blocks, NETS, O])
            raw_rows = raw[:].rearrange("p b (n o) -> p b n o", o=O)
            if turn == 0:
                nc.vector.tensor_mul(logit[group][:], raw_rows, g_for_nets)
            else:
                nc.vector.tensor_mul(raw_rows, raw_rows, g_for_nets)
                nc.vector.tensor_add(logit[group][:], logit[group][:], raw_rows)

            rows = [P, blocks * NETS, O]
            logit_rows = logit[group][:].rearrange("p b n o -> p (b n) o")
            top = small.tile([P, blocks * NETS], F32, name="top")
            nc.vector.tensor_reduce(top[:], logit_rows, axis=AX.X, op=ALU.max)
            prob = small.tile(rows, F32, name="prob")
            nc.vector.tensor_sub(prob[:], logit_rows, top[:].unsqueeze(2).to_broadcast(rows))
            nc.scalar.activation(prob[:], prob[:], ACT.Exp)
            nc.scalar.activation(warm[:], prob[:, 0, 0:1], ACT.Sqrt)
            total = small.tile([P, blocks * NETS], F32, name="total")
            nc.vector.tensor_reduce(total[:], prob[:], axis=AX.X, op=ALU.add)
            nc.vector.reciprocal(total[:], total[:])
            nc.vector.tensor_mul(prob[:], prob[:], total[:].unsqueeze(2).to_broadcast(rows))
            return prob

        def finish(blk, t_ps):
            t_by_capsule = t_ps.rearrange("p (o k) -> p o k", k=K)
            last_sq = small.tile([P, O, K], F32, name="last_sq")
            if blk == BLOCKS - 1:
                nc.vector.tensor_mul(last_sq[:], t_by_capsule, t_by_capsule)
            else:
                nc.scalar.activation(last_sq[:], t_by_capsule, ACT.Square)
            last_r = small.tile([P, O], F32, name="last_r")
            nc.vector.tensor_reduce(last_r[:], last_sq[:], axis=AX.X, op=ALU.add)
            last_g = squash_scale(nc, small, last_r[:], O)
            v = small.tile([P, O, K], F32, name="v")
            nc.vector.tensor_mul(v[:], t_by_capsule, last_g[:].unsqueeze(2).to_broadcast([P, O, K]))
            nc.scalar.activation(window[blk][:].indirect(offsets[:]), v[:].rearrange("p o k -> p (o k)"), ACT.Copy)
            nc.sync.dma_start(out[blk * P : (blk + 1) * P, :], window[blk][:])

        logit = [held.tile([P, len(blocks), NETS, O], F32, name="logit%d" % i) for i, blocks in enumerate(GROUPS)]
        prob = [None, None]
        for turn in range(PASSES):
            for group, blocks in enumerate(GROUPS):
                t_ps = []
                for i, blk in enumerate(blocks):
                    if turn == 0:
                        terms, count = p[blk], NETS
                        if group == 0:
                            terms, count = folded(folded(terms, NETS, 2), NETS // 2, 2), NETS // 4
                        t_ps.append(sum_over_nets(terms, count, eye_over_o)[:])
                        continue
                    block_prob = prob[group][:, i * NETS : (i + 1) * NETS, :]
                    if turn == 1 and blk == SPARED:
                        by_vector = 0
                    elif turn == PASSES - 1 and blk == BLOCKS - 1:
                        by_vector = NETS // 2
                    else:
                        by_vector = NETS
                    terms, count = weighted_votes(blk, block_prob, by_vector), NETS
                    if turn == PASSES - 1 and blk == BLOCKS - 1:
                        for rows in (8, 4, 2):
                            terms = folded(terms, rows, 2 if rows > 2 else 1)
                        t_ps.append(terms[:, 0, :])
                        continue
                    if turn == PASSES - 1 and group == 1:
                        terms, count = folded(terms, NETS, 2), NETS // 2
                    t_ps.append(sum_over_nets(terms, count, eye)[:])
                if turn + 1 < PASSES:
                    raw = small.tile([P, len(blocks), NETS * O], F32, name="raw")
                    r = small.tile([P, len(blocks) * O], F32, name="r")
                    for i, blk in enumerate(blocks):
                        agreement(blk, t_ps[i], raw[:, i, :], r[:, i * O : (i + 1) * O])
                    prob[group] = new_probabilities(group, turn, raw, r)
                else:
                    for i, blk in enumerate(blocks):
                        finish(blk, t_ps[i])
